import numpy as np
import ml_dtypes


def mxq(x, axis, fmt="e4m3"):
    dtype, down = {"e4m3": (ml_dtypes.float8_e4m3fn, 7), "e5m2": (ml_dtypes.float8_e5m2, 14)}[fmt]
    v = np.moveaxis(np.asarray(x, np.float32).astype(ml_dtypes.bfloat16).astype(np.float64), axis, -1)
    blocks = v.reshape(v.shape[:-1] + (-1, 32))
    amax = np.abs(blocks).max(-1, keepdims=True)
    byte = np.maximum(np.where(amax > 0, np.frexp(amax)[1] - 1 + 127, 0) - down, 1)
    scale = np.exp2(byte - 127.0)
    codes = (blocks / scale).astype(np.float32).astype(dtype).astype(np.float64)
    return np.moveaxis((codes * scale).reshape(v.shape), -1, axis)


WIDE = False


def mx_kscale(k):
    if not WIDE:
        return np.ones(k)
    levels = np.array([10, -10, 5, -5, 0])
    a = np.random.permutation(np.resize(levels, k // 512 * 4)).reshape(k // 512, 4)
    idx = np.arange(k)
    return np.exp2(a[idx // 512, idx % 128 // 32])


BF16 = ml_dtypes.bfloat16


def bf(x):
    return np.asarray(x, np.float32).astype(BF16)


def f64(x):
    return np.asarray(x).astype(np.float64)


E2M1 = np.array([0.0, 0.5, 1.0, 1.5, 2.0, 3.0, 4.0, 6.0, -0.0, -0.5, -1.0, -1.5, -2.0, -3.0, -4.0, -6.0])


def pack_weight(w, fmt):
    k, n = w.shape
    w = f64(bf(w)).reshape(k // 32, 32, n)
    amax = np.abs(w).max(1)
    if fmt == "e4m3":
        byte = np.frexp(amax)[1] - 1 + 127 - 7
    else:
        mant, ex = np.frexp(amax / 6.0)
        byte = np.where(mant > 0.5, ex, ex - 1) + 127
    byte = np.clip(np.where(amax > 0, byte, 1), 1, 254)
    scaled = (w * np.exp2(127.0 - byte)[:, None, :]).reshape(k, n).astype(np.float32)
    by_word = np.ascontiguousarray(scaled.reshape(k // 512, 128, 4, n).transpose(0, 1, 3, 2))
    if fmt == "e4m3":
        words = by_word.astype(ml_dtypes.float8_e4m3fn).view(np.uint8)
    else:
        c = by_word.astype(ml_dtypes.float4_e2m1fn).view(np.uint8) & 0xF
        words = c[..., 0::2] | (c[..., 1::2] << 4)
    return np.ascontiguousarray(words), np.ascontiguousarray(byte.astype(np.uint8).reshape(k // 512, 16, n))


def unpack_weight(words, scales, fmt):
    g, p, n, _ = words.shape
    if fmt == "e4m3":
        vals = np.ascontiguousarray(words).view(ml_dtypes.float8_e4m3fn).astype(np.float64)
    else:
        nib = np.empty((g, p, n, 4), np.uint8)
        nib[..., 0::2] = words & 0xF
        nib[..., 1::2] = words >> 4
        vals = E2M1[nib]
    vals = vals * np.repeat(np.exp2(scales.astype(np.float64) - 127.0), 8, axis=1)[..., None]
    return vals.transpose(0, 1, 3, 2).reshape(g * 512, n)

def pack4(w):
    words, scales = pack_weight(w, "e2m1")
    return words.reshape(words.shape[0], 128, -1), scales


def unpack4(words, scales):
    return unpack_weight(words.reshape(words.shape[0], 128, -1, 2), scales, "e2m1")


B, T, C, E, DV, R, G, BLK = 1, 512, 512, 512, 512, 16, 16, 512
BASE = 1e4


def rope(x):
    inv_freq = 1.0 / (BASE ** (f64(np.arange(0, R, 2)) / R))
    ang = f64(np.arange(T))[:, None] * inv_freq[None, :]
    ang = np.repeat(ang, 2, axis=-1)
    cos, sin = np.cos(ang), np.sin(ang)
    xl, xr = x[..., :R], x[..., R:]
    p = xl.reshape(xl.shape[:-1] + (R // 2, 2))
    rot = np.stack((-p[..., 1], p[..., 0]), axis=-1).reshape(xl.shape)
    return np.concatenate([xl * cos + rot * sin, xr], axis=-1)


def setup_inputs():
    s = mx_kscale(C)
    Q_in = bf(np.random.standard_normal((B, T, C)) * s)
    wq_words, wq_scales = pack4(np.random.standard_normal((C, E)) * 0.25 / np.sqrt(C) / s[:, None])
    wk_words, wk_scales = pack4(np.random.standard_normal((C, E)) * 0.25 / np.sqrt(C) / s[:, None])
    return {"Q_in": Q_in,
            "W_Q_words": wq_words, "W_Q_scales": wq_scales,
            "W_K_words": wk_words, "W_K_scales": wk_scales}


def reference(Q_in, W_Q_words, W_Q_scales, W_K_words, W_K_scales):
    xq = mxq(f64(Q_in), 2, "e4m3")
    q = rope(xq @ unpack4(W_Q_words, W_Q_scales))
    k = rope(xq @ unpack4(W_K_words, W_K_scales))
    return q, k

@@ -1,0 +1,169 @@
+import math
+from contextlib import ExitStack
+
+import concourse.mybir as mybir
+from concourse.masks import make_identity
+
+F32 = mybir.dt.float32
+BF16 = mybir.dt.bfloat16
+I32 = mybir.dt.int32
+U8 = mybir.dt.uint8
+U32 = mybir.dt.uint32
+FP8X4 = mybir.dt.float8_e4m3fn_x4
+FP4X4 = mybir.dt.float4_e2m1fn_x4
+ALU = mybir.AluOpType
+ACT = mybir.ActivationFunctionType
+
+P = 128
+PACK = 4
+T = 512
+C = 512
+E = 512
+TILES = T // P
+ROPE = 16
+PAIRS = ROPE // 2
+ROPE_BASE = 10000.0
+ROUND_MAGIC = 1.5 * 2.0**23
+
+FLOPS = 2 * 2 * T * C * E
+
+
+def tile_wqkv_pa_s_kernel(
+    tc, Q_in, W_Q_words, W_Q_scales, W_K_words, W_K_scales, out_0, out_1
+):
+    nc = tc.nc
+    weights = ((W_Q_words, W_Q_scales), (W_K_words, W_K_scales))
+    x_rows = Q_in[0].rearrange("(p i) c -> p i c", i=TILES)
+    out_rows = [o[0].rearrange("(p i) e -> p i e", i=TILES) for o in (out_0, out_1)]
+
+    with ExitStack() as ctx:
+        keep = ctx.enter_context(tc.tile_pool(name="keep", bufs=1))
+        stage = ctx.enter_context(tc.tile_pool(name="stage", bufs=TILES))
+        psum = ctx.enter_context(tc.psum_pool(name="psum", bufs=8))
+
+        x_half = []
+        for h in range(2):
+            x_sb = keep.tile([P, 2, C], BF16, name="x_half%d" % h)
+            nc.scalar.dma_start(out=x_sb[:], in_=x_rows[:, 2 * h : 2 * h + 2, :])
+            x_half.append(x_sb)
+
+        w_planes = keep.tile([P, 2, E], U8, align_bytes=64)
+        nc.vector.memset(w_planes[:].rearrange("p w e -> p (w e)").bitcast(I32), 0)
+        w_words = keep.tile([P, 2, 2 * E], U8, align_bytes=64)
+
+        def load_scales(w):
+            rows = weights[w][1][0].rearrange("(quad r) e -> r quad e", r=4)
+            for r in range(4):
+                nc.sync.dma_start(
+                    out=w_planes[r:P:32, w, :].bitcast(I32), in_=rows[r].bitcast(I32)
+                )
+
+        def load_words(w):
+            nc.sync.dma_start(
+                out=w_words[:, w, :].bitcast(I32), in_=weights[w][0][0].bitcast(I32)
+            )
+
+        load_scales(0)
+        load_words(0)
+        load_words(1)
+        load_scales(1)
+
+        ident = keep.tile([P, P], F32)
+        make_identity(nc, ident[:])
+
+        position = keep.tile([P, TILES], I32)
+        nc.gpsimd.iota(out=position[:], pattern=[[1, TILES]], base=0, channel_multiplier=TILES)
+
+        turns = keep.tile([P, 2, TILES, PAIRS], F32)
+        for j in range(PAIRS):
+            turns_per_position = ROPE_BASE ** (-2.0 * j / ROPE) / (2.0 * math.pi)
+            nc.vector.tensor_scalar(
+                out=turns[:, 0, :, j],
+                in0=position[:],
+                scalar1=turns_per_position,
+                scalar2=None,
+                op0=ALU.mult,
+            )
+        nc.vector.tensor_scalar(
+            out=turns[:, 1], in0=turns[:, 0], scalar1=0.25, scalar2=None, op0=ALU.add
+        )
+        whole = keep.tile([P, 2, TILES, PAIRS], F32)
+        nc.vector.tensor_scalar(
+            out=whole[:],
+            in0=turns[:],
+            scalar1=ROUND_MAGIC,
+            scalar2=ROUND_MAGIC,
+            op0=ALU.add,
+            op1=ALU.subtract,
+        )
+        part = keep.tile([P, 2, TILES, PAIRS], F32)
+        nc.vector.tensor_tensor(out=part[:], in0=turns[:], in1=whole[:], op=ALU.subtract)
+
+        rot = keep.tile([P, TILES, PAIRS, 2, 2], F32)
+        rot_flat = rot[:].rearrange("p i j e m -> p (i j) (e m)")
+        sin_part = part[:, 0].rearrange("p i j -> p (i j)").unsqueeze(2)
+        cos_part = part[:, 1].rearrange("p i j -> p (i j)").unsqueeze(2)
+        nc.scalar.activation(
+            out=rot_flat[:, :, 0:4:3],
+            in_=cos_part.to_broadcast([P, TILES * PAIRS, 2]),
+            func=ACT.Sin,
+            scale=2.0 * math.pi,
+        )
+        nc.scalar.activation(
+            out=rot_flat[:, :, 1:2], in_=sin_part, func=ACT.Sin, scale=-2.0 * math.pi
+        )
+        nc.scalar.activation(
+            out=rot_flat[:, :, 2:3], in_=sin_part, func=ACT.Sin, scale=2.0 * math.pi
+        )
+
+        x_codes = keep.tile([P, TILES, P], U32, align_bytes=64)
+        x_scales = keep.tile([P, TILES, P], U8, align_bytes=64)
+        for i in range(TILES):
+            x_words = x_half[i // 2][:, i % 2, :].bitcast(F32)
+            flipped = psum.tile([P, 2, P], F32, tag="bank")
+            for u in range(2):
+                nc.tensor.transpose(flipped[:, u, :], x_words[:, u : C // 2 : 2], ident[:])
+            grouped = stage.tile([P, P, PACK], BF16, align_bytes=64)
+            grouped_words = (
+                grouped[:].rearrange("p r t -> p (r t)").bitcast(F32).rearrange("p (r u) -> p r u", u=2)
+            )
+            copy_out = nc.vector.tensor_copy if i % 2 == 0 else nc.scalar.copy
+            copy_out(out=grouped_words, in_=flipped[:].rearrange("p u r -> p r u"))
+            nc.vector.quantize_mx(
+                out=x_codes[:, i, :].bitcast(FP8X4),
+                scales=x_scales[:, i, :],
+                in_=grouped[:].rearrange("p r t -> p (r t)"),
+            )
+
+        for w in range(2):
+            result = keep.tile([P, TILES, E], F32, name="result%d" % w)
+            for i in range(TILES):
+                acc = psum.tile([P, E], F32, tag="bank")
+                nc.tensor.matmul_mx(
+                    out=acc[:],
+                    lhsT=x_codes[:, i, :].bitcast(FP8X4),
+                    lhsT_scale=x_scales[:, i, :],
+                    rhs=w_words[:, w, :].bitcast(FP4X4),
+                    rhs_scale=w_planes[:, w, :],
+                    start=True,
+                    stop=True,
+                )
+                products = stage.tile([P, PAIRS, 2, 2], F32)
+                nc.vector.tensor_tensor(
+                    out=products[:],
+                    in0=acc[:, 0:ROPE]
+                    .rearrange("p (j m) -> p j m", m=2)
+                    .unsqueeze(2)
+                    .to_broadcast([P, PAIRS, 2, 2]),
+                    in1=rot[:, i],
+                    op=ALU.mult,
+                )
+                copy_out = nc.scalar.copy if i % 2 == 0 else nc.vector.tensor_copy
+                copy_out(out=result[:, i, ROPE:E], in_=acc[:, ROPE:E])
+                nc.vector.tensor_reduce(
+                    out=result[:, i, 0:ROPE],
+                    in_=products[:].rearrange("p j e m -> p (j e) m"),
+                    axis=mybir.AxisListType.X,
+                    op=ALU.add,
+                )
+                nc.sync.dma_start(out=out_rows[w][:, i, :], in_=result[:, i, :])

@@ -24,6 +24,8 @@ ROPE = 16
 PAIRS = ROPE // 2
 ROPE_BASE = 10000.0
 ROUND_MAGIC = 1.5 * 2.0**23
+HALF = E // 2
+SINGLE_STORES = 2
 
 FLOPS = 2 * 2 * T * C * E
 
@@ -41,38 +43,28 @@ def tile_wqkv_pa_s_kernel(
         stage = ctx.enter_context(tc.tile_pool(name="stage", bufs=TILES))
         psum = ctx.enter_context(tc.psum_pool(name="psum", bufs=8))
 
-        x_half = []
-        for h in range(2):
-            x_sb = keep.tile([P, 2, C], BF16, name="x_half%d" % h)
-            nc.scalar.dma_start(out=x_sb[:], in_=x_rows[:, 2 * h : 2 * h + 2, :])
-            x_half.append(x_sb)
+        x_sb = keep.tile([P, TILES, C], BF16)
+        for first, count in ((0, 1), (1, 1), (2, 2)):
+            nc.sync.dma_start(
+                out=x_sb[:, first : first + count, :], in_=x_rows[:, first : first + count, :]
+            )
 
         w_planes = keep.tile([P, 2, E], U8, align_bytes=64)
         nc.vector.memset(w_planes[:].rearrange("p w e -> p (w e)").bitcast(I32), 0)
         w_words = keep.tile([P, 2, 2 * E], U8, align_bytes=64)
-
-        def load_scales(w):
-            rows = weights[w][1][0].rearrange("(quad r) e -> r quad e", r=4)
+        for w in range(2):
+            words, scales = weights[w]
+            scale_rows = scales[0].rearrange("(quad r) e -> r quad e", r=4)
             for r in range(4):
                 nc.sync.dma_start(
-                    out=w_planes[r:P:32, w, :].bitcast(I32), in_=rows[r].bitcast(I32)
+                    out=w_planes[r:P:32, w, :].bitcast(I32), in_=scale_rows[r].bitcast(I32)
                 )
-
-        def load_words(w):
-            nc.sync.dma_start(
-                out=w_words[:, w, :].bitcast(I32), in_=weights[w][0][0].bitcast(I32)
-            )
-
-        load_scales(0)
-        load_words(0)
-        load_words(1)
-        load_scales(1)
-
-        ident = keep.tile([P, P], F32)
-        make_identity(nc, ident[:])
+            nc.sync.dma_start(out=w_words[:, w, :].bitcast(I32), in_=words[0].bitcast(I32))
 
         position = keep.tile([P, TILES], I32)
         nc.gpsimd.iota(out=position[:], pattern=[[1, TILES]], base=0, channel_multiplier=TILES)
+        ident = keep.tile([P, P], F32)
+        make_identity(nc, ident[:])
 
         turns = keep.tile([P, 2, TILES, PAIRS], F32)
         for j in range(PAIRS):
@@ -118,17 +110,20 @@ def tile_wqkv_pa_s_kernel(
 
         x_codes = keep.tile([P, TILES, P], U32, align_bytes=64)
         x_scales = keep.tile([P, TILES, P], U8, align_bytes=64)
+        flipped = []
         for i in range(TILES):
-            x_words = x_half[i // 2][:, i % 2, :].bitcast(F32)
-            flipped = psum.tile([P, 2, P], F32, tag="bank")
+            x_words = x_sb[:, i, :].bitcast(F32)
+            flipped_i = psum.tile([P, 2, P], F32, tag="bank", name="flipped%d" % i)
             for u in range(2):
-                nc.tensor.transpose(flipped[:, u, :], x_words[:, u : C // 2 : 2], ident[:])
+                nc.tensor.transpose(flipped_i[:, u, :], x_words[:, u : C // 2 : 2], ident[:])
+            flipped.append(flipped_i)
+        for i in range(TILES):
             grouped = stage.tile([P, P, PACK], BF16, align_bytes=64)
             grouped_words = (
                 grouped[:].rearrange("p r t -> p (r t)").bitcast(F32).rearrange("p (r u) -> p r u", u=2)
             )
             copy_out = nc.vector.tensor_copy if i % 2 == 0 else nc.scalar.copy
-            copy_out(out=grouped_words, in_=flipped[:].rearrange("p u r -> p r u"))
+            copy_out(out=grouped_words, in_=flipped[i][:].rearrange("p u r -> p r u"))
             nc.vector.quantize_mx(
                 out=x_codes[:, i, :].bitcast(FP8X4),
                 scales=x_scales[:, i, :],
@@ -138,32 +133,41 @@ def tile_wqkv_pa_s_kernel(
         for w in range(2):
             result = keep.tile([P, TILES, E], F32, name="result%d" % w)
             for i in range(TILES):
-                acc = psum.tile([P, E], F32, tag="bank")
-                nc.tensor.matmul_mx(
-                    out=acc[:],
-                    lhsT=x_codes[:, i, :].bitcast(FP8X4),
-                    lhsT_scale=x_scales[:, i, :],
-                    rhs=w_words[:, w, :].bitcast(FP4X4),
-                    rhs_scale=w_planes[:, w, :],
-                    start=True,
-                    stop=True,
-                )
+                halves = []
+                for h in range(2):
+                    acc = psum.tile([P, HALF], F32, tag="bank", name="acc%d" % h)
+                    nc.tensor.matmul_mx(
+                        out=acc[:],
+                        lhsT=x_codes[:, i, :].bitcast(FP8X4),
+                        lhsT_scale=x_scales[:, i, :],
+                        rhs=w_words[:, w, 2 * HALF * h : 2 * HALF * (h + 1)].bitcast(FP4X4),
+                        rhs_scale=w_planes[:, w, HALF * h : HALF * (h + 1)],
+                        start=True,
+                        stop=True,
+                    )
+                    halves.append(acc)
+                left, right = halves
                 products = stage.tile([P, PAIRS, 2, 2], F32)
                 nc.vector.tensor_tensor(
                     out=products[:],
-                    in0=acc[:, 0:ROPE]
+                    in0=left[:, 0:ROPE]
                     .rearrange("p (j m) -> p j m", m=2)
                     .unsqueeze(2)
                     .to_broadcast([P, PAIRS, 2, 2]),
                     in1=rot[:, i],
                     op=ALU.mult,
                 )
-                copy_out = nc.scalar.copy if i % 2 == 0 else nc.vector.tensor_copy
-                copy_out(out=result[:, i, ROPE:E], in_=acc[:, ROPE:E])
+                nc.scalar.copy(out=result[:, i, HALF:E], in_=right[:])
+                nc.vector.tensor_copy(out=result[:, i, ROPE:HALF], in_=left[:, ROPE:HALF])
                 nc.vector.tensor_reduce(
                     out=result[:, i, 0:ROPE],
                     in_=products[:].rearrange("p j e m -> p (j e) m"),
                     axis=mybir.AxisListType.X,
                     op=ALU.add,
                 )
-                nc.sync.dma_start(out=out_rows[w][:, i, :], in_=result[:, i, :])
+                if w == 0 and i < SINGLE_STORES:
+                    nc.sync.dma_start(out=out_rows[w][:, i, :], in_=result[:, i, :])
+                elif i % 2 == 1:
+                    nc.sync.dma_start(
+                        out=out_rows[w][:, i - 1 : i + 1, :], in_=result[:, i - 1 : i + 1, :]
+                    )

@@ -26,6 +26,8 @@ ROPE_BASE = 10000.0
 ROUND_MAGIC = 1.5 * 2.0**23
 HALF = E // 2
 SINGLE_STORES = 2
+WARM_MATMULS = 3
+WARM_COLUMNS = 256
 
 FLOPS = 2 * 2 * T * C * E
 
@@ -42,6 +44,12 @@ def tile_wqkv_pa_s_kernel(
         keep = ctx.enter_context(tc.tile_pool(name="keep", bufs=1))
         stage = ctx.enter_context(tc.tile_pool(name="stage", bufs=TILES))
         psum = ctx.enter_context(tc.psum_pool(name="psum", bufs=8))
+
+        zeros = keep.tile([P, WARM_COLUMNS], F32)
+        nc.vector.memset(zeros[:], 0.0)
+        unread = psum.tile([P, WARM_COLUMNS], F32, tag="bank")
+        for n in range(WARM_MATMULS):
+            nc.tensor.matmul(unread[:], lhsT=zeros[:, 0:P], rhs=zeros[:], start=True, stop=True)
 
         x_sb = keep.tile([P, TILES, C], BF16)
         for first, count in ((0, 1), (1, 1), (2, 2)):
@@ -64,7 +72,8 @@ def tile_wqkv_pa_s_kernel(
         position = keep.tile([P, TILES], I32)
         nc.gpsimd.iota(out=position[:], pattern=[[1, TILES]], base=0, channel_multiplier=TILES)
         ident = keep.tile([P, P], F32)
-        make_identity(nc, ident[:])
+        nc.vector.memset(ident[:], 0.0)
+        make_identity(nc, ident[:], nomemset=True)
 
         turns = keep.tile([P, 2, TILES, PAIRS], F32)
         for j in range(PAIRS):

@@ -26,8 +26,6 @@ ROPE_BASE = 10000.0
 ROUND_MAGIC = 1.5 * 2.0**23
 HALF = E // 2
 SINGLE_STORES = 2
-WARM_MATMULS = 3
-WARM_COLUMNS = 256
 
 FLOPS = 2 * 2 * T * C * E
 
@@ -44,12 +42,7 @@ def tile_wqkv_pa_s_kernel(
         keep = ctx.enter_context(tc.tile_pool(name="keep", bufs=1))
         stage = ctx.enter_context(tc.tile_pool(name="stage", bufs=TILES))
         psum = ctx.enter_context(tc.psum_pool(name="psum", bufs=8))
-
-        zeros = keep.tile([P, WARM_COLUMNS], F32)
-        nc.vector.memset(zeros[:], 0.0)
-        unread = psum.tile([P, WARM_COLUMNS], F32, tag="bank")
-        for n in range(WARM_MATMULS):
-            nc.tensor.matmul(unread[:], lhsT=zeros[:, 0:P], rhs=zeros[:], start=True, stop=True)
+        ctx.enter_context(tc.manual_schedule())
 
         x_sb = keep.tile([P, TILES, C], BF16)
         for first, count in ((0, 1), (1, 1), (2, 2)):
@@ -72,8 +65,7 @@ def tile_wqkv_pa_s_kernel(
         position = keep.tile([P, TILES], I32)
         nc.gpsimd.iota(out=position[:], pattern=[[1, TILES]], base=0, channel_multiplier=TILES)
         ident = keep.tile([P, P], F32)
-        nc.vector.memset(ident[:], 0.0)
-        make_identity(nc, ident[:], nomemset=True)
+        make_identity(nc, ident[:])
 
         turns = keep.tile([P, 2, TILES, PAIRS], F32)
         for j in range(PAIRS):

@@ -26,6 +26,7 @@ ROPE_BASE = 10000.0
 ROUND_MAGIC = 1.5 * 2.0**23
 HALF = E // 2
 SINGLE_STORES = 2
+WARM_COLUMNS = 384
 
 FLOPS = 2 * 2 * T * C * E
 
@@ -43,6 +44,11 @@ def tile_wqkv_pa_s_kernel(
         stage = ctx.enter_context(tc.tile_pool(name="stage", bufs=TILES))
         psum = ctx.enter_context(tc.psum_pool(name="psum", bufs=8))
         ctx.enter_context(tc.manual_schedule())
+
+        zeros = keep.tile([P, WARM_COLUMNS], F32)
+        nc.vector.memset(zeros[:], 0.0)
+        unread = psum.tile([P, WARM_COLUMNS], F32, tag="bank")
+        nc.tensor.matmul(unread[:], lhsT=zeros[:, 0:P], rhs=zeros[:], start=True, stop=True)
 
         x_sb = keep.tile([P, TILES, C], BF16)
         for first, count in ((0, 1), (1, 1), (2, 2)):

@@ -25,7 +25,6 @@ PAIRS = ROPE // 2
 ROPE_BASE = 10000.0
 ROUND_MAGIC = 1.5 * 2.0**23
 HALF = E // 2
-SINGLE_STORES = 2
 WARM_COLUMNS = 384
 
 FLOPS = 2 * 2 * T * C * E
@@ -51,22 +50,32 @@ def tile_wqkv_pa_s_kernel(
         nc.tensor.matmul(unread[:], lhsT=zeros[:, 0:P], rhs=zeros[:], start=True, stop=True)
 
         x_sb = keep.tile([P, TILES, C], BF16)
-        for first, count in ((0, 1), (1, 1), (2, 2)):
+        w_planes = keep.tile([P, 2, E], U8, align_bytes=64)
+        nc.vector.memset(w_planes[:].rearrange("p w e -> p (w e)").bitcast(I32), 0)
+        w_words = keep.tile([P, 2, 2 * E], U8, align_bytes=64)
+
+        def load_x(first, count):
             nc.sync.dma_start(
                 out=x_sb[:, first : first + count, :], in_=x_rows[:, first : first + count, :]
             )
 
-        w_planes = keep.tile([P, 2, E], U8, align_bytes=64)
-        nc.vector.memset(w_planes[:].rearrange("p w e -> p (w e)").bitcast(I32), 0)
-        w_words = keep.tile([P, 2, 2 * E], U8, align_bytes=64)
-        for w in range(2):
-            words, scales = weights[w]
-            scale_rows = scales[0].rearrange("(quad r) e -> r quad e", r=4)
+        def load_scales(w):
+            scale_rows = weights[w][1][0].rearrange("(quad r) e -> r quad e", r=4)
             for r in range(4):
                 nc.sync.dma_start(
                     out=w_planes[r:P:32, w, :].bitcast(I32), in_=scale_rows[r].bitcast(I32)
                 )
-            nc.sync.dma_start(out=w_words[:, w, :].bitcast(I32), in_=words[0].bitcast(I32))
+
+        def load_words(w):
+            nc.sync.dma_start(out=w_words[:, w, :].bitcast(I32), in_=weights[w][0][0].bitcast(I32))
+
+        load_x(0, 1)
+        load_x(1, 1)
+        load_x(2, 2)
+        load_scales(0)
+        load_words(0)
+        load_scales(1)
+        load_words(1)
 
         position = keep.tile([P, TILES], I32)
         nc.gpsimd.iota(out=position[:], pattern=[[1, TILES]], base=0, channel_multiplier=TILES)
@@ -117,64 +126,89 @@ def tile_wqkv_pa_s_kernel(
 
         x_codes = keep.tile([P, TILES, P], U32, align_bytes=64)
         x_scales = keep.tile([P, TILES, P], U8, align_bytes=64)
-        flipped = []
-        for i in range(TILES):
+        flipped = {}
+        grouped_of = {}
+
+        def transpose_x(i):
             x_words = x_sb[:, i, :].bitcast(F32)
             flipped_i = psum.tile([P, 2, P], F32, tag="bank", name="flipped%d" % i)
             for u in range(2):
                 nc.tensor.transpose(flipped_i[:, u, :], x_words[:, u : C // 2 : 2], ident[:])
-            flipped.append(flipped_i)
-        for i in range(TILES):
+            flipped[i] = flipped_i
+
+        def group_x(i):
             grouped = stage.tile([P, P, PACK], BF16, align_bytes=64)
             grouped_words = (
                 grouped[:].rearrange("p r t -> p (r t)").bitcast(F32).rearrange("p (r u) -> p r u", u=2)
             )
-            copy_out = nc.vector.tensor_copy if i % 2 == 0 else nc.scalar.copy
-            copy_out(out=grouped_words, in_=flipped[i][:].rearrange("p u r -> p r u"))
+            nc.scalar.copy(out=grouped_words, in_=flipped[i][:].rearrange("p u r -> p r u"))
+            grouped_of[i] = grouped
+
+        def quantise_x(i):
             nc.vector.quantize_mx(
                 out=x_codes[:, i, :].bitcast(FP8X4),
                 scales=x_scales[:, i, :],
-                in_=grouped[:].rearrange("p r t -> p (r t)"),
+                in_=grouped_of[i][:].rearrange("p r t -> p (r t)"),
             )
 
-        for w in range(2):
-            result = keep.tile([P, TILES, E], F32, name="result%d" % w)
-            for i in range(TILES):
-                halves = []
-                for h in range(2):
-                    acc = psum.tile([P, HALF], F32, tag="bank", name="acc%d" % h)
-                    nc.tensor.matmul_mx(
-                        out=acc[:],
-                        lhsT=x_codes[:, i, :].bitcast(FP8X4),
-                        lhsT_scale=x_scales[:, i, :],
-                        rhs=w_words[:, w, 2 * HALF * h : 2 * HALF * (h + 1)].bitcast(FP4X4),
-                        rhs_scale=w_planes[:, w, HALF * h : HALF * (h + 1)],
-                        start=True,
-                        stop=True,
-                    )
-                    halves.append(acc)
-                left, right = halves
-                products = stage.tile([P, PAIRS, 2, 2], F32)
-                nc.vector.tensor_tensor(
-                    out=products[:],
-                    in0=left[:, 0:ROPE]
-                    .rearrange("p (j m) -> p j m", m=2)
-                    .unsqueeze(2)
-                    .to_broadcast([P, PAIRS, 2, 2]),
-                    in1=rot[:, i],
-                    op=ALU.mult,
-                )
-                nc.scalar.copy(out=result[:, i, HALF:E], in_=right[:])
-                nc.vector.tensor_copy(out=result[:, i, ROPE:HALF], in_=left[:, ROPE:HALF])
-                nc.vector.tensor_reduce(
-                    out=result[:, i, 0:ROPE],
-                    in_=products[:].rearrange("p j e m -> p (j e) m"),
-                    axis=mybir.AxisListType.X,
-                    op=ALU.add,
-                )
-                if w == 0 and i < SINGLE_STORES:
-                    nc.sync.dma_start(out=out_rows[w][:, i, :], in_=result[:, i, :])
-                elif i % 2 == 1:
-                    nc.sync.dma_start(
-                        out=out_rows[w][:, i - 1 : i + 1, :], in_=result[:, i - 1 : i + 1, :]
-                    )
+        def multiply(w, i, first, width):
+            bank = psum.tile([P, width], F32, tag="bank", name="bank")
+            nc.tensor.matmul_mx(
+                out=bank[:],
+                lhsT=x_codes[:, i, :].bitcast(FP8X4),
+                lhsT_scale=x_scales[:, i, :],
+                rhs=w_words[:, w, 2 * first : 2 * (first + width)].bitcast(FP4X4),
+                rhs_scale=w_planes[:, w, first : first + width],
+                start=True,
+                stop=True,
+            )
+            return bank
+
+        def rope_terms(terms, bank, i):
+            nc.vector.tensor_tensor(
+                out=terms,
+                in0=bank[:, 0:ROPE]
+                .rearrange("p (j m) -> p j m", m=2)
+                .unsqueeze(2)
+                .to_broadcast([P, PAIRS, 2, 2]),
+                in1=rot[:, i],
+                op=ALU.mult,
+            )
+
+        def store(w, i, rows):
+            nc.sync.dma_start(out=out_rows[w][:, i, :], in_=rows)
+
+        def multiply_halves(w, i):
+            return [multiply(w, i, 0, HALF), multiply(w, i, HALF, HALF)]
+
+        def empty_halves(w, i, banks):
+            left, right = banks
+            res = keep.tile([P, E], F32, name="res_%d_%d" % (w, i))
+            terms = stage.tile([P, PAIRS, 2, 2], F32, name="terms")
+            rope_terms(terms[:], left, i)
+            nc.scalar.copy(out=res[:, HALF:E], in_=right[:])
+            nc.vector.tensor_copy(out=res[:, ROPE:HALF], in_=left[:, ROPE:HALF])
+            nc.vector.tensor_reduce(
+                out=res[:, 0:ROPE],
+                in_=terms[:].rearrange("p j e m -> p (j e) m"),
+                axis=mybir.AxisListType.X,
+                op=ALU.add,
+            )
+            store(w, i, res[:])
+
+        for i in range(3):
+            transpose_x(i)
+        for i in range(3):
+            group_x(i)
+        quantise_x(0)
+        quantise_x(1)
+        banks_0 = multiply_halves(0, 0)
+        transpose_x(3)
+        empty_halves(0, 0, banks_0)
+        group_x(3)
+        quantise_x(2)
+        banks_1 = multiply_halves(0, 1)
+        empty_halves(0, 1, banks_1)
+        quantise_x(3)
+        for w, i in ((0, 2), (0, 3), (1, 0), (1, 1), (1, 2), (1, 3)):
+            empty_halves(w, i, multiply_halves(w, i))

@@ -109,20 +109,15 @@ def tile_wqkv_pa_s_kernel(
 
         rot = keep.tile([P, TILES, PAIRS, 2, 2], F32)
         rot_flat = rot[:].rearrange("p i j e m -> p (i j) (e m)")
-        sin_part = part[:, 0].rearrange("p i j -> p (i j)").unsqueeze(2)
-        cos_part = part[:, 1].rearrange("p i j -> p (i j)").unsqueeze(2)
-        nc.scalar.activation(
-            out=rot_flat[:, :, 0:4:3],
-            in_=cos_part.to_broadcast([P, TILES * PAIRS, 2]),
-            func=ACT.Sin,
-            scale=2.0 * math.pi,
+        waves = keep.tile([P, 2, TILES, PAIRS], F32)
+        nc.scalar.activation(out=waves[:], in_=part[:], func=ACT.Sin, scale=2.0 * math.pi)
+        sin_part = waves[:, 0].rearrange("p i j -> p (i j)").unsqueeze(2)
+        cos_part = waves[:, 1].rearrange("p i j -> p (i j)").unsqueeze(2)
+        nc.vector.tensor_copy(out=rot_flat[:, :, 0:4:3], in_=cos_part.to_broadcast([P, TILES * PAIRS, 2]))
+        nc.vector.tensor_scalar(
+            out=rot_flat[:, :, 1:2], in0=sin_part, scalar1=-1.0, scalar2=None, op0=ALU.mult
         )
-        nc.scalar.activation(
-            out=rot_flat[:, :, 1:2], in_=sin_part, func=ACT.Sin, scale=-2.0 * math.pi
-        )
-        nc.scalar.activation(
-            out=rot_flat[:, :, 2:3], in_=sin_part, func=ACT.Sin, scale=2.0 * math.pi
-        )
+        nc.vector.tensor_copy(out=rot_flat[:, :, 2:3], in_=sin_part)
 
         x_codes = keep.tile([P, TILES, P], U32, align_bytes=64)
         x_scales = keep.tile([P, TILES, P], U8, align_bytes=64)
@@ -196,14 +191,13 @@ def tile_wqkv_pa_s_kernel(
             )
             store(w, i, res[:])
 
-        for i in range(3):
+        for i in range(TILES):
             transpose_x(i)
         for i in range(3):
             group_x(i)
         quantise_x(0)
         quantise_x(1)
         banks_0 = multiply_halves(0, 0)
-        transpose_x(3)
         empty_halves(0, 0, banks_0)
         group_x(3)
         quantise_x(2)

@@ -176,19 +176,25 @@ def tile_wqkv_pa_s_kernel(
         def multiply_halves(w, i):
             return [multiply(w, i, 0, HALF), multiply(w, i, HALF, HALF)]
 
-        def empty_halves(w, i, banks):
+        def empty_halves(w, i, banks, sum_on_vector=False):
             left, right = banks
             res = keep.tile([P, E], F32, name="res_%d_%d" % (w, i))
             terms = stage.tile([P, PAIRS, 2, 2], F32, name="terms")
             rope_terms(terms[:], left, i)
             nc.scalar.copy(out=res[:, HALF:E], in_=right[:])
             nc.vector.tensor_copy(out=res[:, ROPE:HALF], in_=left[:, ROPE:HALF])
-            nc.vector.tensor_reduce(
-                out=res[:, 0:ROPE],
-                in_=terms[:].rearrange("p j e m -> p (j e) m"),
-                axis=mybir.AxisListType.X,
-                op=ALU.add,
-            )
+            pairs_of_terms = terms[:].rearrange("p j e m -> p (j e) m")
+            if sum_on_vector:
+                nc.vector.tensor_reduce(
+                    out=res[:, 0:ROPE], in_=pairs_of_terms, axis=mybir.AxisListType.X, op=ALU.add
+                )
+            else:
+                nc.gpsimd.tensor_tensor(
+                    out=res[:, 0:ROPE],
+                    in0=pairs_of_terms[:, :, 0],
+                    in1=pairs_of_terms[:, :, 1],
+                    op=ALU.add,
+                )
             store(w, i, res[:])
 
         for i in range(TILES):
@@ -198,11 +204,12 @@ def tile_wqkv_pa_s_kernel(
         quantise_x(0)
         quantise_x(1)
         banks_0 = multiply_halves(0, 0)
-        empty_halves(0, 0, banks_0)
+        empty_halves(0, 0, banks_0, sum_on_vector=True)
         group_x(3)
         quantise_x(2)
         banks_1 = multiply_halves(0, 1)
         empty_halves(0, 1, banks_1)
         quantise_x(3)
-        for w, i in ((0, 2), (0, 3), (1, 0), (1, 1), (1, 2), (1, 3)):
+        for w, i in ((0, 2), (0, 3), (1, 0), (1, 1), (1, 2)):
             empty_halves(w, i, multiply_halves(w, i))
+        empty_halves(1, 3, multiply_halves(1, 3), sum_on_vector=True)

import math
from contextlib import ExitStack

import concourse.mybir as mybir
from concourse.masks import make_identity

F32 = mybir.dt.float32
BF16 = mybir.dt.bfloat16
I32 = mybir.dt.int32
U8 = mybir.dt.uint8
U32 = mybir.dt.uint32
FP8X4 = mybir.dt.float8_e4m3fn_x4
FP4X4 = mybir.dt.float4_e2m1fn_x4
ALU = mybir.AluOpType
ACT = mybir.ActivationFunctionType

P = 128
PACK = 4
T = 512
C = 512
E = 512
TILES = T // P
ROPE = 16
PAIRS = ROPE // 2
ROPE_BASE = 10000.0
ROUND_MAGIC = 1.5 * 2.0**23
HALF = E // 2
WARM_COLUMNS = 384

FLOPS = 2 * 2 * T * C * E


def tile_wqkv_pa_s_kernel(
    tc, Q_in, W_Q_words, W_Q_scales, W_K_words, W_K_scales, out_0, out_1
):
    nc = tc.nc
    weights = ((W_Q_words, W_Q_scales), (W_K_words, W_K_scales))
    x_rows = Q_in[0].rearrange("(p i) c -> p i c", i=TILES)
    out_rows = [o[0].rearrange("(p i) e -> p i e", i=TILES) for o in (out_0, out_1)]

    with ExitStack() as ctx:
        keep = ctx.enter_context(tc.tile_pool(name="keep", bufs=1))
        stage = ctx.enter_context(tc.tile_pool(name="stage", bufs=TILES))
        psum = ctx.enter_context(tc.psum_pool(name="psum", bufs=8))
        ctx.enter_context(tc.manual_schedule())

        zeros = keep.tile([P, WARM_COLUMNS], F32)
        nc.vector.memset(zeros[:], 0.0)
        unread = psum.tile([P, WARM_COLUMNS], F32, tag="bank")
        nc.tensor.matmul(unread[:], lhsT=zeros[:, 0:P], rhs=zeros[:], start=True, stop=True)

        x_sb = keep.tile([P, TILES, C], BF16)
        w_planes = keep.tile([P, 2, E], U8, align_bytes=64)
        nc.vector.memset(w_planes[:].rearrange("p w e -> p (w e)").bitcast(I32), 0)
        w_words = keep.tile([P, 2, 2 * E], U8, align_bytes=64)

        def load_x(first, count):
            nc.sync.dma_start(
                out=x_sb[:, first : first + count, :], in_=x_rows[:, first : first + count, :]
            )

        def load_scales(w):
            scale_rows = weights[w][1][0].rearrange("(quad r) e -> r quad e", r=4)
            for r in range(4):
                nc.sync.dma_start(
                    out=w_planes[r:P:32, w, :].bitcast(I32), in_=scale_rows[r].bitcast(I32)
                )

        def load_words(w):
            nc.sync.dma_start(out=w_words[:, w, :].bitcast(I32), in_=weights[w][0][0].bitcast(I32))

        load_x(0, 1)
        load_x(1, 1)
        load_x(2, 2)
        load_scales(0)
        load_words(0)
        load_scales(1)
        load_words(1)

        position = keep.tile([P, TILES], I32)
        nc.gpsimd.iota(out=position[:], pattern=[[1, TILES]], base=0, channel_multiplier=TILES)
        ident = keep.tile([P, P], F32)
        make_identity(nc, ident[:])

        turns = keep.tile([P, 2, TILES, PAIRS], F32)
        for j in range(PAIRS):
            turns_per_position = ROPE_BASE ** (-2.0 * j / ROPE) / (2.0 * math.pi)
            nc.vector.tensor_scalar(
                out=turns[:, 0, :, j],
                in0=position[:],
                scalar1=turns_per_position,
                scalar2=None,
                op0=ALU.mult,
            )
        nc.vector.tensor_scalar(
            out=turns[:, 1], in0=turns[:, 0], scalar1=0.25, scalar2=None, op0=ALU.add
        )
        whole = keep.tile([P, 2, TILES, PAIRS], F32)
        nc.vector.tensor_scalar(
            out=whole[:],
            in0=turns[:],
            scalar1=ROUND_MAGIC,
            scalar2=ROUND_MAGIC,
            op0=ALU.add,
            op1=ALU.subtract,
        )
        part = keep.tile([P, 2, TILES, PAIRS], F32)
        nc.vector.tensor_tensor(out=part[:], in0=turns[:], in1=whole[:], op=ALU.subtract)

        rot = keep.tile([P, TILES, PAIRS, 2, 2], F32)
        rot_flat = rot[:].rearrange("p i j e m -> p (i j) (e m)")
        waves = keep.tile([P, 2, TILES, PAIRS], F32)
        nc.scalar.activation(out=waves[:], in_=part[:], func=ACT.Sin, scale=2.0 * math.pi)
        sin_part = waves[:, 0].rearrange("p i j -> p (i j)").unsqueeze(2)
        cos_part = waves[:, 1].rearrange("p i j -> p (i j)").unsqueeze(2)
        nc.vector.tensor_copy(out=rot_flat[:, :, 0:4:3], in_=cos_part.to_broadcast([P, TILES * PAIRS, 2]))
        nc.vector.tensor_scalar(
            out=rot_flat[:, :, 1:2], in0=sin_part, scalar1=-1.0, scalar2=None, op0=ALU.mult
        )
        nc.vector.tensor_copy(out=rot_flat[:, :, 2:3], in_=sin_part)

        x_codes = keep.tile([P, TILES, P], U32, align_bytes=64)
        x_scales = keep.tile([P, TILES, P], U8, align_bytes=64)
        flipped = {}
        grouped_of = {}

        def transpose_x(i):
            x_words = x_sb[:, i, :].bitcast(F32)
            flipped_i = psum.tile([P, 2, P], F32, tag="bank", name="flipped%d" % i)
            for u in range(2):
                nc.tensor.transpose(flipped_i[:, u, :], x_words[:, u : C // 2 : 2], ident[:])
            flipped[i] = flipped_i

        def group_x(i):
            grouped = stage.tile([P, P, PACK], BF16, align_bytes=64)
            grouped_words = (
                grouped[:].rearrange("p r t -> p (r t)").bitcast(F32).rearrange("p (r u) -> p r u", u=2)
            )
            nc.scalar.copy(out=grouped_words, in_=flipped[i][:].rearrange("p u r -> p r u"))
            grouped_of[i] = grouped

        def quantise_x(i):
            nc.vector.quantize_mx(
                out=x_codes[:, i, :].bitcast(FP8X4),
                scales=x_scales[:, i, :],
                in_=grouped_of[i][:].rearrange("p r t -> p (r t)"),
            )

        def multiply(w, i, first, width):
            bank = psum.tile([P, width], F32, tag="bank", name="bank")
            nc.tensor.matmul_mx(
                out=bank[:],
                lhsT=x_codes[:, i, :].bitcast(FP8X4),
                lhsT_scale=x_scales[:, i, :],
                rhs=w_words[:, w, 2 * first : 2 * (first + width)].bitcast(FP4X4),
                rhs_scale=w_planes[:, w, first : first + width],
                start=True,
                stop=True,
            )
            return bank

        def rope_terms(terms, bank, i):
            nc.vector.tensor_tensor(
                out=terms,
                in0=bank[:, 0:ROPE]
                .rearrange("p (j m) -> p j m", m=2)
                .unsqueeze(2)
                .to_broadcast([P, PAIRS, 2, 2]),
                in1=rot[:, i],
                op=ALU.mult,
            )

        def store(w, i, rows):
            nc.sync.dma_start(out=out_rows[w][:, i, :], in_=rows)

        def multiply_halves(w, i):
            return [multiply(w, i, 0, HALF), multiply(w, i, HALF, HALF)]

        def empty_halves(w, i, banks, sum_on_vector=False):
            left, right = banks
            res = keep.tile([P, E], F32, name="res_%d_%d" % (w, i))
            terms = stage.tile([P, PAIRS, 2, 2], F32, name="terms")
            rope_terms(terms[:], left, i)
            nc.scalar.copy(out=res[:, HALF:E], in_=right[:])
            nc.vector.tensor_copy(out=res[:, ROPE:HALF], in_=left[:, ROPE:HALF])
            pairs_of_terms = terms[:].rearrange("p j e m -> p (j e) m")
            if sum_on_vector:
                nc.vector.tensor_reduce(
                    out=res[:, 0:ROPE], in_=pairs_of_terms, axis=mybir.AxisListType.X, op=ALU.add
                )
            else:
                nc.gpsimd.tensor_tensor(
                    out=res[:, 0:ROPE],
                    in0=pairs_of_terms[:, :, 0],
                    in1=pairs_of_terms[:, :, 1],
                    op=ALU.add,
                )
            store(w, i, res[:])

        for i in range(TILES):
            transpose_x(i)
        for i in range(3):
            group_x(i)
        quantise_x(0)
        quantise_x(1)
        banks_0 = multiply_halves(0, 0)
        empty_halves(0, 0, banks_0, sum_on_vector=True)
        group_x(3)
        quantise_x(2)
        banks_1 = multiply_halves(0, 1)
        empty_halves(0, 1, banks_1)
        quantise_x(3)
        for w, i in ((0, 2), (0, 3), (1, 0), (1, 1), (1, 2)):
            empty_halves(w, i, multiply_halves(w, i))
        empty_halves(1, 3, multiply_halves(1, 3), sum_on_vector=True)
